import numpy as np
import ml_dtypes


def mxq(x, axis, fmt="e4m3"):
    dtype, down = {"e4m3": (ml_dtypes.float8_e4m3fn, 7), "e5m2": (ml_dtypes.float8_e5m2, 14)}[fmt]
    v = np.moveaxis(np.asarray(x, np.float32).astype(ml_dtypes.bfloat16).astype(np.float64), axis, -1)
    blocks = v.reshape(v.shape[:-1] + (-1, 32))
    amax = np.abs(blocks).max(-1, keepdims=True)
    byte = np.maximum(np.where(amax > 0, np.frexp(amax)[1] - 1 + 127, 0) - down, 1)
    scale = np.exp2(byte - 127.0)
    codes = (blocks / scale).astype(np.float32).astype(dtype).astype(np.float64)
    return np.moveaxis((codes * scale).reshape(v.shape), -1, axis)


WIDE = False


def mx_kscale(k):
    if not WIDE:
        return np.ones(k)
    levels = np.array([20, -20, 10, -10, 0])
    a = np.random.permutation(np.resize(levels, k // 512 * 4)).reshape(k // 512, 4)
    idx = np.arange(k)
    return np.exp2(a[idx // 512, idx % 128 // 32])


BF16 = ml_dtypes.bfloat16


def bf(x):
    return np.asarray(x, np.float32).astype(BF16)


def f64(x):
    return np.asarray(x).astype(np.float64)


B, K, N = 2048, 512, 1024
NACT = 4


def act_deriv(y):
    rows, cols = y.shape
    y3 = y.reshape(rows, cols // NACT, NACT)
    c3 = np.cos(y3[..., 3])
    d = np.stack(
        [np.ones_like(y3[..., 0]),
         -np.sin(y3[..., 1]),
         np.cos(y3[..., 2]),
         1.0 / (c3 * c3)],
        axis=-1,
    )
    return d.reshape(rows, cols)


def setup_inputs():
    s = mx_kscale(B)[:, None]
    h = np.tile(np.array([1.0, 1.0, 1.0, 0.5]), N // NACT)
    x0 = bf(np.random.standard_normal((B, K)))
    weight = bf(np.random.uniform(-1.0, 1.0, (N, K)) / np.sqrt(K) * h[:, None])
    g = bf(np.random.standard_normal((B, N)) * np.exp2(np.random.randint(-12, 1, (B, 1))) / s)
    y = f64(x0) @ f64(weight).T
    return {"x": bf(f64(x0) * s), "weight": weight, "y": np.asarray(y, np.float32), "grad_out": g}


def reference(x, weight, y, grad_out):
    dy = f64(grad_out) * act_deriv(f64(y))
    return mxq(dy, 0, "e5m2").T @ mxq(f64(x), 0, "e4m3")

@@ -1,0 +1,171 @@
+from contextlib import ExitStack
+
+import concourse.mybir as mybir
+
+F32 = mybir.dt.float32
+BF16 = mybir.dt.bfloat16
+U32 = mybir.dt.uint32
+U8 = mybir.dt.uint8
+E4M3X4 = mybir.dt.float8_e4m3fn_x4
+E5M2X4 = mybir.dt.float8_e5m2_x4
+ACT = mybir.ActivationFunctionType
+ALU = mybir.AluOpType
+
+P = 128
+PACK = 4
+K_PASS = P * PACK
+TOKENS = 2048
+PASSES = TOKENS // K_PASS
+COLS = 1024
+CLASSES = 4
+CB = COLS // CLASSES
+FEAT = 512
+HALVES = CB // P
+RUN = 4
+
+FLOPS = 2 * TOKENS * COLS * FEAT
+BYTES = TOKENS * COLS * 4 + TOKENS * COLS * 2 + TOKENS * FEAT * 2 + COLS * FEAT * 4
+
+
+def by_token(ap):
+    return ap.rearrange("p j (m i) -> p m j i", i=RUN)
+
+
+def by_column(ap):
+    return ap.rearrange("p (m i) j -> p m j i", i=RUN)
+
+
+def tile_mylayerfunc_v_kernel(tc, x, weight, y, grad_out, out):
+    nc = tc.nc
+    y_dram = y.rearrange("(t p j) n -> t p j n", p=P, j=PACK)
+    g_dram = grad_out.rearrange("(t p j) n -> t p j n", p=P, j=PACK)
+    x_dram = x.rearrange("(t p j) k -> t p j k", p=P, j=PACK)
+    out_dram = out.rearrange("(cb c) k -> c cb k", c=CLASSES)
+
+    with ExitStack() as stack:
+        stack.enter_context(tc.manual_schedule())
+        loads = stack.enter_context(tc.tile_pool(name="loads", bufs=1))
+        keep = stack.enter_context(tc.tile_pool(name="keep", bufs=1))
+        work = stack.enter_context(tc.tile_pool(name="work", bufs=2))
+        results = stack.enter_context(tc.tile_pool(name="results", bufs=4))
+        psum = stack.enter_context(tc.psum_pool(name="psum", bufs=1))
+
+        one = keep.tile([P, 1], F32, name="one")
+        nc.vector.memset(one[:], 1.0)
+
+        y_sb = [loads.tile([P, PACK, COLS], F32, name="y%d" % t) for t in range(PASSES)]
+        g_sb = [loads.tile([P, PACK, COLS], BF16, name="g%d" % t) for t in range(PASSES)]
+        x_sb = [loads.tile([P, PACK, FEAT], BF16, name="x%d" % t) for t in range(PASSES)]
+        for t in range(PASSES):
+            for j0 in range(0, PACK, 2):
+                nc.sync.dma_start(out=y_sb[t][:, j0 : j0 + 2, :], in_=y_dram[t][:, j0 : j0 + 2, :])
+            nc.sync.dma_start(out=g_sb[t][:], in_=g_dram[t])
+            nc.sync.dma_start(out=x_sb[t][:], in_=x_dram[t])
+
+        dy_codes = keep.tile([P, PASSES, CLASSES, CB], U32, name="dy_codes", align_bytes=64)
+        dy_scales = keep.tile([P, PASSES, CLASSES, CB], U8, name="dy_scales", align_bytes=64)
+        x_codes = keep.tile([P, PASSES, FEAT], U32, name="x_codes", align_bytes=64)
+        x_scales = keep.tile([P, PASSES, FEAT], U8, name="x_scales", align_bytes=64)
+        cos4 = [keep.tile([P, PACK, CB], F32, name="cos4_%d" % t) for t in range(PASSES)]
+        acc = [
+            [psum.tile([P, FEAT], F32, name="acc%d%d" % (c, h)) for h in range(HALVES)]
+            for c in range(CLASSES)
+        ]
+        dy_bf = {}
+
+        def column_class(ap, c):
+            return ap.rearrange("p j (cb c) -> p j cb c", c=CLASSES)[:, :, :, c]
+
+        def quantise_dy(t, c):
+            nc.vector.quantize_mx(
+                out=dy_codes[:, t, c, :].bitcast(E5M2X4),
+                scales=dy_scales[:, t, c, :],
+                in_=dy_bf[(t, c)].rearrange("p cb j -> p (cb j)"),
+            )
+            for h in range(HALVES):
+                cols = slice(h * P, (h + 1) * P)
+                nc.tensor.matmul_mx(
+                    out=acc[c][h][:],
+                    lhsT=dy_codes[:, t, c, cols].bitcast(E5M2X4),
+                    lhsT_scale=dy_scales[:, t, c, cols],
+                    rhs=x_codes[:, t, :].bitcast(E4M3X4),
+                    rhs_scale=x_scales[:, t, :],
+                    start=(t == 0),
+                    stop=(t == PASSES - 1),
+                )
+
+        def store(c, h, engine_copy):
+            res = results.tile([P, FEAT], F32, name="res")
+            engine_copy(out=res[:], in_=acc[c][h][:])
+            nc.sync.dma_start(out=out_dram[c][h * P : (h + 1) * P, :], in_=res[:])
+
+        for t in range(PASSES):
+            y4 = y_sb[t][:].rearrange("p j (cb c) -> p j cb c", c=CLASSES)
+            sin13 = work.tile([P, PACK, CB, 2], F32, name="sin13")
+            sq3 = work.tile([P, PACK, CB], F32, name="sq3")
+            for j0 in range(0, PACK, 2):
+                js = slice(j0, j0 + 2)
+                nc.scalar.activation(out=sin13[:, js, :, :], in_=y4[:, js, :, 1::2], func=ACT.Sin, scale=-1.0)
+                nc.scalar.activation(out=sq3[:, js, :], in_=sin13[:, js, :, 1], func=ACT.Square)
+                nc.scalar.activation(
+                    out=cos4[t][:, js, :], in_=sq3[:, js, :], func=ACT.Square, scale=-1.0, bias=one[:]
+                )
+            half2 = work.tile([P, CB, PACK], F32, name="half2")
+            nc.scalar.activation(
+                out=half2[:], in_=y4[:, :, :, 2].rearrange("p j cb -> p cb j"), func=ACT.Sin, scale=0.5
+            )
+
+            x_bf = work.tile([P, FEAT, PACK], BF16, name="x_bf", align_bytes=64)
+            nc.vector.tensor_copy(out=by_column(x_bf[:]), in_=by_token(x_sb[t][:]))
+            if t > 0:
+                quantise_dy(t - 1, 2)
+            dy012 = work.tile([P, 3, CB, PACK], BF16, name="dy012", align_bytes=64)
+            for c in range(3):
+                dy_bf[(t, c)] = dy012[:, c, :, :]
+            nc.vector.tensor_copy(out=by_column(dy_bf[(t, 0)]), in_=by_token(column_class(g_sb[t][:], 0)))
+            nc.vector.quantize_mx(
+                out=x_codes[:, t, :].bitcast(E4M3X4),
+                scales=x_scales[:, t, :],
+                in_=x_bf[:].rearrange("p k j -> p (k j)"),
+            )
+            nc.vector.tensor_tensor(
+                out=by_column(dy_bf[(t, 1)]),
+                in0=by_token(sin13[:, :, :, 0]),
+                in1=by_token(column_class(g_sb[t][:], 1)),
+                op=ALU.mult,
+            )
+            quantise_dy(t, 0)
+            nc.vector.scalar_tensor_tensor(
+                out=half2[:], in0=half2[:], scalar=-2.0, in1=half2[:], op0=ALU.mult, op1=ALU.mult
+            )
+            quantise_dy(t, 1)
+            nc.vector.scalar_tensor_tensor(
+                out=dy_bf[(t, 2)],
+                in0=half2[:],
+                scalar=1.0,
+                in1=column_class(g_sb[t][:], 2).rearrange("p j cb -> p cb j"),
+                op0=ALU.add,
+                op1=ALU.mult,
+            )
+
+        for t in range(PASSES):
+            nc.scalar.activation(out=cos4[t][:], in_=cos4[t][:], func=ACT.Abs_reciprocal_sqrt)
+        for t in range(PASSES):
+            dy3 = work.tile([P, CB, PACK], BF16, name="dy3", align_bytes=64)
+            dy_bf[(t, 3)] = dy3[:]
+            nc.vector.tensor_tensor(
+                out=by_column(dy3[:]),
+                in0=by_token(cos4[t][:]),
+                in1=by_token(column_class(g_sb[t][:], 3)),
+                op=ALU.mult,
+            )
+            if t == 0:
+                quantise_dy(PASSES - 1, 2)
+            else:
+                quantise_dy(t - 1, 3)
+        for c in range(3):
+            for h in range(HALVES):
+                store(c, h, nc.scalar.copy)
+        quantise_dy(PASSES - 1, 3)
+        store(3, 0, nc.vector.tensor_copy)
+        store(3, 1, nc.scalar.copy)

@@ -47,6 +47,7 @@ def tile_mylayerfunc_v_kernel(tc, x, weight, y, grad_out, out):
         loads = stack.enter_context(tc.tile_pool(name="loads", bufs=1))
         keep = stack.enter_context(tc.tile_pool(name="keep", bufs=1))
         work = stack.enter_context(tc.tile_pool(name="work", bufs=2))
+        dy_pool = stack.enter_context(tc.tile_pool(name="dy_pool", bufs=3))
         results = stack.enter_context(tc.tile_pool(name="results", bufs=4))
         psum = stack.enter_context(tc.psum_pool(name="psum", bufs=1))
 
@@ -57,10 +58,10 @@ def tile_mylayerfunc_v_kernel(tc, x, weight, y, grad_out, out):
         g_sb = [loads.tile([P, PACK, COLS], BF16, name="g%d" % t) for t in range(PASSES)]
         x_sb = [loads.tile([P, PACK, FEAT], BF16, name="x%d" % t) for t in range(PASSES)]
         for t in range(PASSES):
+            nc.sync.dma_start(out=x_sb[t][:], in_=x_dram[t])
             for j0 in range(0, PACK, 2):
                 nc.sync.dma_start(out=y_sb[t][:, j0 : j0 + 2, :], in_=y_dram[t][:, j0 : j0 + 2, :])
             nc.sync.dma_start(out=g_sb[t][:], in_=g_dram[t])
-            nc.sync.dma_start(out=x_sb[t][:], in_=x_dram[t])
 
         dy_codes = keep.tile([P, PASSES, CLASSES, CB], U32, name="dy_codes", align_bytes=64)
         dy_scales = keep.tile([P, PASSES, CLASSES, CB], U8, name="dy_scales", align_bytes=64)
@@ -99,73 +100,72 @@ def tile_mylayerfunc_v_kernel(tc, x, weight, y, grad_out, out):
             engine_copy(out=res[:], in_=acc[c][h][:])
             nc.sync.dma_start(out=out_dram[c][h * P : (h + 1) * P, :], in_=res[:])
 
-        for t in range(PASSES):
+        def sines_and_cos4(t, sin13, j0):
             y4 = y_sb[t][:].rearrange("p j (cb c) -> p j cb c", c=CLASSES)
-            sin13 = work.tile([P, PACK, CB, 2], F32, name="sin13")
-            sq3 = work.tile([P, PACK, CB], F32, name="sq3")
-            for j0 in range(0, PACK, 2):
-                js = slice(j0, j0 + 2)
-                nc.scalar.activation(out=sin13[:, js, :, :], in_=y4[:, js, :, 1::2], func=ACT.Sin, scale=-1.0)
-                nc.scalar.activation(out=sq3[:, js, :], in_=sin13[:, js, :, 1], func=ACT.Square)
-                nc.scalar.activation(
-                    out=cos4[t][:, js, :], in_=sq3[:, js, :], func=ACT.Square, scale=-1.0, bias=one[:]
+            js = slice(j0, j0 + 2)
+            sq3 = work.tile([P, 2, CB], F32, name="sq3")
+            nc.scalar.activation(out=sin13[:, js, :, :], in_=y4[:, js, :, 1::2], func=ACT.Sin, scale=-1.0)
+            nc.scalar.activation(out=sq3[:], in_=sin13[:, js, :, 1], func=ACT.Square)
+            nc.scalar.activation(out=cos4[t][:, js, :], in_=sq3[:], func=ACT.Square, scale=-1.0, bias=one[:])
+
+        factor = {}
+
+        def make_dy(t, c):
+            dy = dy_pool.tile([P, CB, PACK], BF16, name="dy", align_bytes=64)
+            dy_bf[(t, c)] = dy[:]
+            g_c = column_class(g_sb[t][:], c)
+            if c == 0:
+                nc.vector.tensor_copy(out=by_column(dy[:]), in_=by_token(g_c))
+            elif c == 2:
+                nc.vector.scalar_tensor_tensor(
+                    out=dy[:],
+                    in0=factor[(t, c)],
+                    scalar=1.0,
+                    in1=g_c.rearrange("p j cb -> p cb j"),
+                    op0=ALU.add,
+                    op1=ALU.mult,
                 )
-            half2 = work.tile([P, CB, PACK], F32, name="half2")
-            nc.scalar.activation(
-                out=half2[:], in_=y4[:, :, :, 2].rearrange("p j cb -> p cb j"), func=ACT.Sin, scale=0.5
-            )
-
-            x_bf = work.tile([P, FEAT, PACK], BF16, name="x_bf", align_bytes=64)
-            nc.vector.tensor_copy(out=by_column(x_bf[:]), in_=by_token(x_sb[t][:]))
-            if t > 0:
-                quantise_dy(t - 1, 2)
-            dy012 = work.tile([P, 3, CB, PACK], BF16, name="dy012", align_bytes=64)
-            for c in range(3):
-                dy_bf[(t, c)] = dy012[:, c, :, :]
-            nc.vector.tensor_copy(out=by_column(dy_bf[(t, 0)]), in_=by_token(column_class(g_sb[t][:], 0)))
-            nc.vector.quantize_mx(
-                out=x_codes[:, t, :].bitcast(E4M3X4),
-                scales=x_scales[:, t, :],
-                in_=x_bf[:].rearrange("p k j -> p (k j)"),
-            )
-            nc.vector.tensor_tensor(
-                out=by_column(dy_bf[(t, 1)]),
-                in0=by_token(sin13[:, :, :, 0]),
-                in1=by_token(column_class(g_sb[t][:], 1)),
-                op=ALU.mult,
-            )
-            quantise_dy(t, 0)
-            nc.vector.scalar_tensor_tensor(
-                out=half2[:], in0=half2[:], scalar=-2.0, in1=half2[:], op0=ALU.mult, op1=ALU.mult
-            )
-            quantise_dy(t, 1)
-            nc.vector.scalar_tensor_tensor(
-                out=dy_bf[(t, 2)],
-                in0=half2[:],
-                scalar=1.0,
-                in1=column_class(g_sb[t][:], 2).rearrange("p j cb -> p cb j"),
-                op0=ALU.add,
-                op1=ALU.mult,
-            )
-
-        for t in range(PASSES):
-            nc.scalar.activation(out=cos4[t][:], in_=cos4[t][:], func=ACT.Abs_reciprocal_sqrt)
-        for t in range(PASSES):
-            dy3 = work.tile([P, CB, PACK], BF16, name="dy3", align_bytes=64)
-            dy_bf[(t, 3)] = dy3[:]
-            nc.vector.tensor_tensor(
-                out=by_column(dy3[:]),
-                in0=by_token(cos4[t][:]),
-                in1=by_token(column_class(g_sb[t][:], 3)),
-                op=ALU.mult,
-            )
-            if t == 0:
-                quantise_dy(PASSES - 1, 2)
             else:
-                quantise_dy(t - 1, 3)
-        for c in range(3):
+                nc.vector.tensor_tensor(
+                    out=by_column(dy[:]), in0=by_token(factor[(t, c)]), in1=by_token(g_c), op=ALU.mult
+                )
+
+        jobs = [(t, c) for t in range(PASSES) for c in (0, 2, 1)] + [(t, 3) for t in range(PASSES)]
+        for n, (t, c) in enumerate(jobs):
+            if c == 0:
+                sin13 = work.tile([P, PACK, CB, 2], F32, name="sin13")
+                half2 = work.tile([P, CB, PACK], F32, name="half2")
+                sines_and_cos4(t, sin13, 0)
+                nc.scalar.activation(
+                    out=half2[:],
+                    in_=column_class(y_sb[t][:], 2).rearrange("p j cb -> p cb j"),
+                    func=ACT.Sin,
+                    scale=0.5,
+                )
+                sines_and_cos4(t, sin13, 2)
+                factor[(t, 1)] = sin13[:, :, :, 0]
+                factor[(t, 2)] = half2[:]
+                factor[(t, 3)] = cos4[t][:]
+
+                x_bf = work.tile([P, FEAT, PACK], BF16, name="x_bf", align_bytes=64)
+                nc.vector.tensor_copy(out=by_column(x_bf[:]), in_=by_token(x_sb[t][:]))
+                nc.vector.scalar_tensor_tensor(
+                    out=half2[:], in0=half2[:], scalar=-2.0, in1=half2[:], op0=ALU.mult, op1=ALU.mult
+                )
+                nc.vector.quantize_mx(
+                    out=x_codes[:, t, :].bitcast(E4M3X4),
+                    scales=x_scales[:, t, :],
+                    in_=x_bf[:].rearrange("p k j -> p (k j)"),
+                )
+            if (t, c) == (0, 3):
+                for u in range(PASSES):
+                    nc.scalar.activation(out=cos4[u][:], in_=cos4[u][:], func=ACT.Abs_reciprocal_sqrt)
+            make_dy(t, c)
+            if n > 0:
+                quantise_dy(*jobs[n - 1])
+        for c in (0, 2, 1):
             for h in range(HALVES):
                 store(c, h, nc.scalar.copy)
-        quantise_dy(PASSES - 1, 3)
+        quantise_dy(*jobs[-1])
         store(3, 0, nc.vector.tensor_copy)
         store(3, 1, nc.scalar.copy)

@@ -58,9 +58,9 @@ def tile_mylayerfunc_v_kernel(tc, x, weight, y, grad_out, out):
         g_sb = [loads.tile([P, PACK, COLS], BF16, name="g%d" % t) for t in range(PASSES)]
         x_sb = [loads.tile([P, PACK, FEAT], BF16, name="x%d" % t) for t in range(PASSES)]
         for t in range(PASSES):
-            nc.sync.dma_start(out=x_sb[t][:], in_=x_dram[t])
             for j0 in range(0, PACK, 2):
                 nc.sync.dma_start(out=y_sb[t][:, j0 : j0 + 2, :], in_=y_dram[t][:, j0 : j0 + 2, :])
+            nc.sync.dma_start(out=x_sb[t][:], in_=x_dram[t])
             nc.sync.dma_start(out=g_sb[t][:], in_=g_dram[t])
 
         dy_codes = keep.tile([P, PASSES, CLASSES, CB], U32, name="dy_codes", align_bytes=64)
@@ -100,15 +100,31 @@ def tile_mylayerfunc_v_kernel(tc, x, weight, y, grad_out, out):
             engine_copy(out=res[:], in_=acc[c][h][:])
             nc.sync.dma_start(out=out_dram[c][h * P : (h + 1) * P, :], in_=res[:])
 
-        def sines_and_cos4(t, sin13, j0):
-            y4 = y_sb[t][:].rearrange("p j (cb c) -> p j cb c", c=CLASSES)
-            js = slice(j0, j0 + 2)
-            sq3 = work.tile([P, 2, CB], F32, name="sq3")
-            nc.scalar.activation(out=sin13[:, js, :, :], in_=y4[:, js, :, 1::2], func=ACT.Sin, scale=-1.0)
-            nc.scalar.activation(out=sq3[:], in_=sin13[:, js, :, 1], func=ACT.Square)
-            nc.scalar.activation(out=cos4[t][:, js, :], in_=sq3[:], func=ACT.Square, scale=-1.0, bias=one[:])
-
         factor = {}
+        waiting = []
+
+        def quantise_waiting():
+            if waiting:
+                quantise_dy(*waiting.pop())
+
+        def scalar_pass(t):
+            y4 = y_sb[t][:].rearrange("p j (cb c) -> p j cb c", c=CLASSES)
+            sin13 = work.tile([P, PACK, CB, 2], F32, name="sin13")
+            half_y2 = work.tile([P, PACK, CB], F32, name="half_y2")
+            half2 = work.tile([P, CB, PACK], F32, name="half2")
+            for j0 in range(0, PACK, 2):
+                js = slice(j0, j0 + 2)
+                nc.gpsimd.tensor_scalar(
+                    out=half_y2[:, js, :], in0=y4[:, js, :, 2], scalar1=0.5, scalar2=0.0, op0=ALU.mult, op1=ALU.add
+                )
+                sq3 = work.tile([P, 2, CB], F32, name="sq3")
+                nc.scalar.activation(out=sin13[:, js, :, :], in_=y4[:, js, :, 1::2], func=ACT.Sin, scale=-1.0)
+                nc.scalar.activation(out=sq3[:], in_=sin13[:, js, :, 1], func=ACT.Square)
+                nc.scalar.activation(out=cos4[t][:, js, :], in_=sq3[:], func=ACT.Square, scale=-1.0, bias=one[:])
+            nc.scalar.activation(out=half2[:], in_=half_y2[:].rearrange("p j cb -> p cb j"), func=ACT.Sin)
+            factor[(t, 1)] = sin13[:, :, :, 0]
+            factor[(t, 2)] = half2[:]
+            factor[(t, 3)] = cos4[t][:]
 
         def make_dy(t, c):
             dy = dy_pool.tile([P, CB, PACK], BF16, name="dy", align_bytes=64)
@@ -129,43 +145,33 @@ def tile_mylayerfunc_v_kernel(tc, x, weight, y, grad_out, out):
                 nc.vector.tensor_tensor(
                     out=by_column(dy[:]), in0=by_token(factor[(t, c)]), in1=by_token(g_c), op=ALU.mult
                 )
+            quantise_waiting()
+            waiting.append((t, c))
 
-        jobs = [(t, c) for t in range(PASSES) for c in (0, 2, 1)] + [(t, 3) for t in range(PASSES)]
-        for n, (t, c) in enumerate(jobs):
-            if c == 0:
-                sin13 = work.tile([P, PACK, CB, 2], F32, name="sin13")
-                half2 = work.tile([P, CB, PACK], F32, name="half2")
-                sines_and_cos4(t, sin13, 0)
-                nc.scalar.activation(
-                    out=half2[:],
-                    in_=column_class(y_sb[t][:], 2).rearrange("p j cb -> p cb j"),
-                    func=ACT.Sin,
-                    scale=0.5,
-                )
-                sines_and_cos4(t, sin13, 2)
-                factor[(t, 1)] = sin13[:, :, :, 0]
-                factor[(t, 2)] = half2[:]
-                factor[(t, 3)] = cos4[t][:]
-
-                x_bf = work.tile([P, FEAT, PACK], BF16, name="x_bf", align_bytes=64)
-                nc.vector.tensor_copy(out=by_column(x_bf[:]), in_=by_token(x_sb[t][:]))
-                nc.vector.scalar_tensor_tensor(
-                    out=half2[:], in0=half2[:], scalar=-2.0, in1=half2[:], op0=ALU.mult, op1=ALU.mult
-                )
-                nc.vector.quantize_mx(
-                    out=x_codes[:, t, :].bitcast(E4M3X4),
-                    scales=x_scales[:, t, :],
-                    in_=x_bf[:].rearrange("p k j -> p (k j)"),
-                )
-            if (t, c) == (0, 3):
-                for u in range(PASSES):
-                    nc.scalar.activation(out=cos4[u][:], in_=cos4[u][:], func=ACT.Abs_reciprocal_sqrt)
-            make_dy(t, c)
-            if n > 0:
-                quantise_dy(*jobs[n - 1])
-        for c in (0, 2, 1):
+        for t in range(PASSES):
+            scalar_pass(t)
+            x_bf = work.tile([P, FEAT, PACK], BF16, name="x_bf", align_bytes=64)
+            nc.vector.tensor_copy(out=by_column(x_bf[:]), in_=by_token(x_sb[t][:]))
+            quantise_waiting()
+            nc.vector.quantize_mx(
+                out=x_codes[:, t, :].bitcast(E4M3X4),
+                scales=x_scales[:, t, :],
+                in_=x_bf[:].rearrange("p k j -> p (k j)"),
+            )
+            make_dy(t, 0)
+            make_dy(t, 1)
+            nc.vector.scalar_tensor_tensor(
+                out=factor[(t, 2)], in0=factor[(t, 2)], scalar=-2.0, in1=factor[(t, 2)], op0=ALU.mult, op1=ALU.mult
+            )
+            quantise_waiting()
+            make_dy(t, 2)
+        for t in range(PASSES):
+            nc.scalar.activation(out=cos4[t][:], in_=cos4[t][:], func=ACT.Abs_reciprocal_sqrt)
+        for t in range(PASSES):
+            make_dy(t, 3)
+        for c in range(3):
             for h in range(HALVES):
                 store(c, h, nc.scalar.copy)
-        quantise_dy(*jobs[-1])
+        quantise_waiting()
         store(3, 0, nc.vector.tensor_copy)
         store(3, 1, nc.scalar.copy)

@@ -110,18 +110,16 @@ def tile_mylayerfunc_v_kernel(tc, x, weight, y, grad_out, out):
         def scalar_pass(t):
             y4 = y_sb[t][:].rearrange("p j (cb c) -> p j cb c", c=CLASSES)
             sin13 = work.tile([P, PACK, CB, 2], F32, name="sin13")
-            half_y2 = work.tile([P, PACK, CB], F32, name="half_y2")
             half2 = work.tile([P, CB, PACK], F32, name="half2")
             for j0 in range(0, PACK, 2):
                 js = slice(j0, j0 + 2)
-                nc.gpsimd.tensor_scalar(
-                    out=half_y2[:, js, :], in0=y4[:, js, :, 2], scalar1=0.5, scalar2=0.0, op0=ALU.mult, op1=ALU.add
-                )
                 sq3 = work.tile([P, 2, CB], F32, name="sq3")
                 nc.scalar.activation(out=sin13[:, js, :, :], in_=y4[:, js, :, 1::2], func=ACT.Sin, scale=-1.0)
                 nc.scalar.activation(out=sq3[:], in_=sin13[:, js, :, 1], func=ACT.Square)
                 nc.scalar.activation(out=cos4[t][:, js, :], in_=sq3[:], func=ACT.Square, scale=-1.0, bias=one[:])
-            nc.scalar.activation(out=half2[:], in_=half_y2[:].rearrange("p j cb -> p cb j"), func=ACT.Sin)
+            nc.scalar.activation(
+                out=half2[:], in_=y4[:, :, :, 2].rearrange("p j cb -> p cb j"), func=ACT.Sin, scale=0.5
+            )
             factor[(t, 1)] = sin13[:, :, :, 0]
             factor[(t, 2)] = half2[:]
             factor[(t, 3)] = cos4[t][:]

@@ -1,9 +1,11 @@
+import math
 from contextlib import ExitStack
 
 import concourse.mybir as mybir
 
 F32 = mybir.dt.float32
 BF16 = mybir.dt.bfloat16
+I32 = mybir.dt.int32
 U32 = mybir.dt.uint32
 U8 = mybir.dt.uint8
 E4M3X4 = mybir.dt.float8_e4m3fn_x4
@@ -53,6 +55,8 @@ def tile_mylayerfunc_v_kernel(tc, x, weight, y, grad_out, out):
 
         one = keep.tile([P, 1], F32, name="one")
         nc.vector.memset(one[:], 1.0)
+        half_pi = keep.tile([P, 1], F32, name="half_pi")
+        nc.vector.tensor_scalar(out=half_pi[:], in0=one[:], scalar1=math.pi / 2, scalar2=None, op0=ALU.mult)
 
         y_sb = [loads.tile([P, PACK, COLS], F32, name="y%d" % t) for t in range(PASSES)]
         g_sb = [loads.tile([P, PACK, COLS], BF16, name="g%d" % t) for t in range(PASSES)]
@@ -110,18 +114,16 @@ def tile_mylayerfunc_v_kernel(tc, x, weight, y, grad_out, out):
         def scalar_pass(t):
             y4 = y_sb[t][:].rearrange("p j (cb c) -> p j cb c", c=CLASSES)
             sin13 = work.tile([P, PACK, CB, 2], F32, name="sin13")
-            half2 = work.tile([P, CB, PACK], F32, name="half2")
+            cos2 = work.tile([P, PACK, CB], F32, name="cos2")
             for j0 in range(0, PACK, 2):
                 js = slice(j0, j0 + 2)
                 sq3 = work.tile([P, 2, CB], F32, name="sq3")
                 nc.scalar.activation(out=sin13[:, js, :, :], in_=y4[:, js, :, 1::2], func=ACT.Sin, scale=-1.0)
                 nc.scalar.activation(out=sq3[:], in_=sin13[:, js, :, 1], func=ACT.Square)
                 nc.scalar.activation(out=cos4[t][:, js, :], in_=sq3[:], func=ACT.Square, scale=-1.0, bias=one[:])
-            nc.scalar.activation(
-                out=half2[:], in_=y4[:, :, :, 2].rearrange("p j cb -> p cb j"), func=ACT.Sin, scale=0.5
-            )
+            nc.scalar.activation(out=cos2[:], in_=abs2[t], func=ACT.Sin, scale=-1.0, bias=half_pi[:])
             factor[(t, 1)] = sin13[:, :, :, 0]
-            factor[(t, 2)] = half2[:]
+            factor[(t, 2)] = cos2[:]
             factor[(t, 3)] = cos4[t][:]
 
         def make_dy(t, c):
@@ -130,15 +132,6 @@ def tile_mylayerfunc_v_kernel(tc, x, weight, y, grad_out, out):
             g_c = column_class(g_sb[t][:], c)
             if c == 0:
                 nc.vector.tensor_copy(out=by_column(dy[:]), in_=by_token(g_c))
-            elif c == 2:
-                nc.vector.scalar_tensor_tensor(
-                    out=dy[:],
-                    in0=factor[(t, c)],
-                    scalar=1.0,
-                    in1=g_c.rearrange("p j cb -> p cb j"),
-                    op0=ALU.add,
-                    op1=ALU.mult,
-                )
             else:
                 nc.vector.tensor_tensor(
                     out=by_column(dy[:]), in0=by_token(factor[(t, c)]), in1=by_token(g_c), op=ALU.mult
@@ -146,7 +139,18 @@ def tile_mylayerfunc_v_kernel(tc, x, weight, y, grad_out, out):
             quantise_waiting()
             waiting.append((t, c))
 
+        abs2 = {}
+
+        def absolute_pass(t):
+            a = work.tile([P, PACK, CB], F32, name="abs2")
+            abs2[t] = a[:]
+            y4i = y_sb[t][:].bitcast(I32).rearrange("p j (cb c) -> p j cb c", c=CLASSES)
+            nc.vector.tensor_scalar(
+                out=a[:].bitcast(I32), in0=y4i[:, :, :, 2], scalar1=0x7FFFFFFF, scalar2=None, op0=ALU.bitwise_and
+            )
+
         for t in range(PASSES):
+            absolute_pass(t)
             scalar_pass(t)
             x_bf = work.tile([P, FEAT, PACK], BF16, name="x_bf", align_bytes=64)
             nc.vector.tensor_copy(out=by_column(x_bf[:]), in_=by_token(x_sb[t][:]))
@@ -158,10 +162,6 @@ def tile_mylayerfunc_v_kernel(tc, x, weight, y, grad_out, out):
             )
             make_dy(t, 0)
             make_dy(t, 1)
-            nc.vector.scalar_tensor_tensor(
-                out=factor[(t, 2)], in0=factor[(t, 2)], scalar=-2.0, in1=factor[(t, 2)], op0=ALU.mult, op1=ALU.mult
-            )
-            quantise_waiting()
             make_dy(t, 2)
         for t in range(PASSES):
             nc.scalar.activation(out=cos4[t][:], in_=cos4[t][:], func=ACT.Abs_reciprocal_sqrt)

@@ -50,7 +50,7 @@ def tile_mylayerfunc_v_kernel(tc, x, weight, y, grad_out, out):
         keep = stack.enter_context(tc.tile_pool(name="keep", bufs=1))
         work = stack.enter_context(tc.tile_pool(name="work", bufs=2))
         dy_pool = stack.enter_context(tc.tile_pool(name="dy_pool", bufs=3))
-        results = stack.enter_context(tc.tile_pool(name="results", bufs=4))
+        results = stack.enter_context(tc.tile_pool(name="results", bufs=8))
         psum = stack.enter_context(tc.psum_pool(name="psum", bufs=1))
 
         one = keep.tile([P, 1], F32, name="one")

@@ -49,7 +49,7 @@ def tile_mylayerfunc_v_kernel(tc, x, weight, y, grad_out, out):
         loads = stack.enter_context(tc.tile_pool(name="loads", bufs=1))
         keep = stack.enter_context(tc.tile_pool(name="keep", bufs=1))
         work = stack.enter_context(tc.tile_pool(name="work", bufs=2))
-        dy_pool = stack.enter_context(tc.tile_pool(name="dy_pool", bufs=3))
+        dy_pool = stack.enter_context(tc.tile_pool(name="dy_pool", bufs=8))
         results = stack.enter_context(tc.tile_pool(name="results", bufs=8))
         psum = stack.enter_context(tc.psum_pool(name="psum", bufs=1))
 
@@ -61,32 +61,89 @@ def tile_mylayerfunc_v_kernel(tc, x, weight, y, grad_out, out):
         y_sb = [loads.tile([P, PACK, COLS], F32, name="y%d" % t) for t in range(PASSES)]
         g_sb = [loads.tile([P, PACK, COLS], BF16, name="g%d" % t) for t in range(PASSES)]
         x_sb = [loads.tile([P, PACK, FEAT], BF16, name="x%d" % t) for t in range(PASSES)]
-        for t in range(PASSES):
-            for j0 in range(0, PACK, 2):
-                nc.sync.dma_start(out=y_sb[t][:, j0 : j0 + 2, :], in_=y_dram[t][:, j0 : j0 + 2, :])
+        FIRST, SECOND = slice(0, 2), slice(2, 4)
+
+        def load_y(t, js):
+            nc.sync.dma_start(out=y_sb[t][:, js, :], in_=y_dram[t][:, js, :])
+
+        def load_x(t):
             nc.sync.dma_start(out=x_sb[t][:], in_=x_dram[t])
+
+        def load_g(t):
             nc.sync.dma_start(out=g_sb[t][:], in_=g_dram[t])
+
+        load_y(0, FIRST)
+        load_y(0, SECOND)
+        load_g(0)
+        load_y(1, FIRST)
+        load_x(0)
+        load_y(1, SECOND)
+        load_x(1)
+        load_x(2)
+        load_g(1)
+        load_y(2, FIRST)
+        load_y(2, SECOND)
+        load_g(2)
+        load_y(3, FIRST)
+        load_y(3, SECOND)
+        load_x(3)
+        load_g(3)
 
         dy_codes = keep.tile([P, PASSES, CLASSES, CB], U32, name="dy_codes", align_bytes=64)
         dy_scales = keep.tile([P, PASSES, CLASSES, CB], U8, name="dy_scales", align_bytes=64)
         x_codes = keep.tile([P, PASSES, FEAT], U32, name="x_codes", align_bytes=64)
         x_scales = keep.tile([P, PASSES, FEAT], U8, name="x_scales", align_bytes=64)
-        cos4 = [keep.tile([P, PACK, CB], F32, name="cos4_%d" % t) for t in range(PASSES)]
+        factor3 = [keep.tile([P, PACK, CB], F32, name="factor3_%d" % t) for t in range(PASSES)]
         acc = [
             [psum.tile([P, FEAT], F32, name="acc%d%d" % (c, h)) for h in range(HALVES)]
             for c in range(CLASSES)
         ]
-        dy_bf = {}
 
-        def column_class(ap, c):
-            return ap.rearrange("p j (cb c) -> p j cb c", c=CLASSES)[:, :, :, c]
+        abs2, sin13, cos2, x_bf = {}, {}, {}, {}
 
-        def quantise_dy(t, c):
-            nc.vector.quantize_mx(
-                out=dy_codes[:, t, c, :].bitcast(E5M2X4),
-                scales=dy_scales[:, t, c, :],
-                in_=dy_bf[(t, c)].rearrange("p cb j -> p (cb j)"),
+        def sines(t, js):
+            if js == FIRST:
+                abs2[t] = work.tile([P, PACK, CB], F32, name="abs2")
+                sin13[t] = work.tile([P, PACK, CB, 2], F32, name="sin13")
+                cos2[t] = work.tile([P, PACK, CB], F32, name="cos2")
+            y4 = y_sb[t][:].rearrange("p j (cb c) -> p j cb c", c=CLASSES)
+            y4i = y_sb[t][:].bitcast(I32).rearrange("p j (cb c) -> p j cb c", c=CLASSES)
+            nc.vector.tensor_scalar(
+                out=abs2[t][:, js, :].bitcast(I32), in0=y4i[:, js, :, 2], scalar1=0x7FFFFFFF, scalar2=None, op0=ALU.bitwise_and
             )
+            nc.scalar.activation(out=sin13[t][:, js, :, :], in_=y4[:, js, :, 1::2], func=ACT.Sin, scale=-1.0)
+            nc.scalar.activation(
+                out=cos2[t][:, js, :], in_=abs2[t][:, js, :], func=ACT.Sin, scale=-1.0, bias=half_pi[:]
+            )
+            nc.scalar.activation(out=factor3[t][:, js, :], in_=sin13[t][:, js, :, 1], func=ACT.Square)
+
+        def fourth_power(t):
+            for js in (FIRST, SECOND):
+                nc.scalar.activation(
+                    out=factor3[t][:, js, :], in_=factor3[t][:, js, :], func=ACT.Square, scale=-1.0, bias=one[:]
+                )
+
+        def reciprocal(t):
+            nc.scalar.activation(out=factor3[t][:], in_=factor3[t][:], func=ACT.Abs_reciprocal_sqrt)
+
+        def regroup_x(t):
+            x_bf[t] = work.tile([P, FEAT, PACK], BF16, name="x_bf", align_bytes=64)
+            nc.vector.tensor_copy(out=by_column(x_bf[t][:]), in_=by_token(x_sb[t][:]))
+
+        made = []
+        held = []
+
+        def make_dy(t, c):
+            dy = dy_pool.tile([P, CB, PACK], BF16, name="dy", align_bytes=64)
+            g_c = g_sb[t][:].rearrange("p j (cb c) -> p j cb c", c=CLASSES)[:, :, :, c]
+            if c == 0:
+                nc.vector.tensor_copy(out=by_column(dy[:]), in_=by_token(g_c))
+            else:
+                factor = (sin13[t][:, :, :, 0], cos2[t][:], factor3[t][:])[c - 1]
+                nc.vector.tensor_tensor(out=by_column(dy[:]), in0=by_token(factor), in1=by_token(g_c), op=ALU.mult)
+            made.append((t, c, dy))
+
+        def multiply(t, c):
             for h in range(HALVES):
                 cols = slice(h * P, (h + 1) * P)
                 nc.tensor.matmul_mx(
@@ -99,77 +156,91 @@ def tile_mylayerfunc_v_kernel(tc, x, weight, y, grad_out, out):
                     stop=(t == PASSES - 1),
                 )
 
+        x_ready = set()
+
+        def quantise_dy():
+            t, c, dy = made.pop(0)
+            nc.vector.quantize_mx(
+                out=dy_codes[:, t, c, :].bitcast(E5M2X4),
+                scales=dy_scales[:, t, c, :],
+                in_=dy[:].rearrange("p cb j -> p (cb j)"),
+            )
+            if t in x_ready:
+                multiply(t, c)
+            else:
+                held.append((t, c))
+
+        def quantise_x(t):
+            nc.vector.quantize_mx(
+                out=x_codes[:, t, :].bitcast(E4M3X4),
+                scales=x_scales[:, t, :],
+                in_=x_bf[t][:].rearrange("p k j -> p (k j)"),
+            )
+            x_ready.add(t)
+            while held:
+                multiply(*held.pop(0))
+
         def store(c, h, engine_copy):
             res = results.tile([P, FEAT], F32, name="res")
             engine_copy(out=res[:], in_=acc[c][h][:])
             nc.sync.dma_start(out=out_dram[c][h * P : (h + 1) * P, :], in_=res[:])
 
-        factor = {}
-        waiting = []
+        def make_first_three(t):
+            for c in range(3):
+                make_dy(t, c)
 
-        def quantise_waiting():
-            if waiting:
-                quantise_dy(*waiting.pop())
-
-        def scalar_pass(t):
-            y4 = y_sb[t][:].rearrange("p j (cb c) -> p j cb c", c=CLASSES)
-            sin13 = work.tile([P, PACK, CB, 2], F32, name="sin13")
-            cos2 = work.tile([P, PACK, CB], F32, name="cos2")
-            for j0 in range(0, PACK, 2):
-                js = slice(j0, j0 + 2)
-                sq3 = work.tile([P, 2, CB], F32, name="sq3")
-                nc.scalar.activation(out=sin13[:, js, :, :], in_=y4[:, js, :, 1::2], func=ACT.Sin, scale=-1.0)
-                nc.scalar.activation(out=sq3[:], in_=sin13[:, js, :, 1], func=ACT.Square)
-                nc.scalar.activation(out=cos4[t][:, js, :], in_=sq3[:], func=ACT.Square, scale=-1.0, bias=one[:])
-            nc.scalar.activation(out=cos2[:], in_=abs2[t], func=ACT.Sin, scale=-1.0, bias=half_pi[:])
-            factor[(t, 1)] = sin13[:, :, :, 0]
-            factor[(t, 2)] = cos2[:]
-            factor[(t, 3)] = cos4[t][:]
-
-        def make_dy(t, c):
-            dy = dy_pool.tile([P, CB, PACK], BF16, name="dy", align_bytes=64)
-            dy_bf[(t, c)] = dy[:]
-            g_c = column_class(g_sb[t][:], c)
-            if c == 0:
-                nc.vector.tensor_copy(out=by_column(dy[:]), in_=by_token(g_c))
-            else:
-                nc.vector.tensor_tensor(
-                    out=by_column(dy[:]), in0=by_token(factor[(t, c)]), in1=by_token(g_c), op=ALU.mult
-                )
-            quantise_waiting()
-            waiting.append((t, c))
-
-        abs2 = {}
-
-        def absolute_pass(t):
-            a = work.tile([P, PACK, CB], F32, name="abs2")
-            abs2[t] = a[:]
-            y4i = y_sb[t][:].bitcast(I32).rearrange("p j (cb c) -> p j cb c", c=CLASSES)
-            nc.vector.tensor_scalar(
-                out=a[:].bitcast(I32), in0=y4i[:, :, :, 2], scalar1=0x7FFFFFFF, scalar2=None, op0=ALU.bitwise_and
-            )
-
-        for t in range(PASSES):
-            absolute_pass(t)
-            scalar_pass(t)
-            x_bf = work.tile([P, FEAT, PACK], BF16, name="x_bf", align_bytes=64)
-            nc.vector.tensor_copy(out=by_column(x_bf[:]), in_=by_token(x_sb[t][:]))
-            quantise_waiting()
-            nc.vector.quantize_mx(
-                out=x_codes[:, t, :].bitcast(E4M3X4),
-                scales=x_scales[:, t, :],
-                in_=x_bf[:].rearrange("p k j -> p (k j)"),
-            )
-            make_dy(t, 0)
-            make_dy(t, 1)
-            make_dy(t, 2)
-        for t in range(PASSES):
-            nc.scalar.activation(out=cos4[t][:], in_=cos4[t][:], func=ACT.Abs_reciprocal_sqrt)
-        for t in range(PASSES):
-            make_dy(t, 3)
-        for c in range(3):
+        sines(0, FIRST)
+        sines(0, SECOND)
+        fourth_power(0)
+        make_first_three(0)
+        sines(1, FIRST)
+        regroup_x(0)
+        quantise_dy()
+        quantise_dy()
+        quantise_x(0)
+        sines(1, SECOND)
+        fourth_power(1)
+        reciprocal(0)
+        reciprocal(1)
+        quantise_dy()
+        regroup_x(1)
+        regroup_x(2)
+        quantise_x(1)
+        quantise_x(2)
+        make_first_three(1)
+        sines(2, FIRST)
+        make_dy(0, 3)
+        sines(2, SECOND)
+        fourth_power(2)
+        quantise_dy()
+        make_dy(1, 3)
+        quantise_dy()
+        make_first_three(2)
+        sines(3, FIRST)
+        quantise_dy()
+        quantise_dy()
+        quantise_dy()
+        sines(3, SECOND)
+        fourth_power(3)
+        reciprocal(2)
+        reciprocal(3)
+        quantise_dy()
+        quantise_dy()
+        regroup_x(3)
+        quantise_dy()
+        quantise_x(3)
+        make_first_three(3)
+        quantise_dy()
+        quantise_dy()
+        quantise_dy()
+        for c in range(2):
             for h in range(HALVES):
                 store(c, h, nc.scalar.copy)
-        quantise_waiting()
+        make_dy(2, 3)
+        make_dy(3, 3)
+        quantise_dy()
+        store(2, 0, nc.vector.tensor_copy)
+        store(2, 1, nc.scalar.copy)
+        quantise_dy()
         store(3, 0, nc.vector.tensor_copy)
         store(3, 1, nc.scalar.copy)

@@ -49,7 +49,7 @@ def tile_mylayerfunc_v_kernel(tc, x, weight, y, grad_out, out):
         loads = stack.enter_context(tc.tile_pool(name="loads", bufs=1))
         keep = stack.enter_context(tc.tile_pool(name="keep", bufs=1))
         work = stack.enter_context(tc.tile_pool(name="work", bufs=2))
-        dy_pool = stack.enter_context(tc.tile_pool(name="dy_pool", bufs=8))
+        dy_pool = stack.enter_context(tc.tile_pool(name="dy_pool", bufs=6))
         results = stack.enter_context(tc.tile_pool(name="results", bufs=8))
         psum = stack.enter_context(tc.psum_pool(name="psum", bufs=1))
 
@@ -79,15 +79,12 @@ def tile_mylayerfunc_v_kernel(tc, x, weight, y, grad_out, out):
         load_x(0)
         load_y(1, SECOND)
         load_x(1)
-        load_x(2)
         load_g(1)
-        load_y(2, FIRST)
-        load_y(2, SECOND)
-        load_g(2)
-        load_y(3, FIRST)
-        load_y(3, SECOND)
-        load_x(3)
-        load_g(3)
+        for t in (2, 3):
+            load_y(t, FIRST)
+            load_y(t, SECOND)
+            load_x(t)
+            load_g(t)
 
         dy_codes = keep.tile([P, PASSES, CLASSES, CB], U32, name="dy_codes", align_bytes=64)
         dy_scales = keep.tile([P, PASSES, CLASSES, CB], U8, name="dy_scales", align_bytes=64)
@@ -101,27 +98,32 @@ def tile_mylayerfunc_v_kernel(tc, x, weight, y, grad_out, out):
 
         abs2, sin13, cos2, x_bf = {}, {}, {}, {}
 
-        def sines(t, js):
+        def absolute(t, js):
             if js == FIRST:
                 abs2[t] = work.tile([P, PACK, CB], F32, name="abs2")
                 sin13[t] = work.tile([P, PACK, CB, 2], F32, name="sin13")
                 cos2[t] = work.tile([P, PACK, CB], F32, name="cos2")
-            y4 = y_sb[t][:].rearrange("p j (cb c) -> p j cb c", c=CLASSES)
             y4i = y_sb[t][:].bitcast(I32).rearrange("p j (cb c) -> p j cb c", c=CLASSES)
             nc.vector.tensor_scalar(
                 out=abs2[t][:, js, :].bitcast(I32), in0=y4i[:, js, :, 2], scalar1=0x7FFFFFFF, scalar2=None, op0=ALU.bitwise_and
             )
+
+        def sine(t, js):
+            y4 = y_sb[t][:].rearrange("p j (cb c) -> p j cb c", c=CLASSES)
             nc.scalar.activation(out=sin13[t][:, js, :, :], in_=y4[:, js, :, 1::2], func=ACT.Sin, scale=-1.0)
+
+        def cosine(t, js):
             nc.scalar.activation(
                 out=cos2[t][:, js, :], in_=abs2[t][:, js, :], func=ACT.Sin, scale=-1.0, bias=half_pi[:]
             )
+
+        def square(t, js):
             nc.scalar.activation(out=factor3[t][:, js, :], in_=sin13[t][:, js, :, 1], func=ACT.Square)
 
-        def fourth_power(t):
-            for js in (FIRST, SECOND):
-                nc.scalar.activation(
-                    out=factor3[t][:, js, :], in_=factor3[t][:, js, :], func=ACT.Square, scale=-1.0, bias=one[:]
-                )
+        def fourth_power(t, js):
+            nc.scalar.activation(
+                out=factor3[t][:, js, :], in_=factor3[t][:, js, :], func=ACT.Square, scale=-1.0, bias=one[:]
+            )
 
         def reciprocal(t):
             nc.scalar.activation(out=factor3[t][:], in_=factor3[t][:], func=ACT.Abs_reciprocal_sqrt)
@@ -132,19 +134,23 @@ def tile_mylayerfunc_v_kernel(tc, x, weight, y, grad_out, out):
 
         made = []
         held = []
+        dy_tiles = {}
 
-        def make_dy(t, c):
-            dy = dy_pool.tile([P, CB, PACK], BF16, name="dy", align_bytes=64)
-            g_c = g_sb[t][:].rearrange("p j (cb c) -> p j cb c", c=CLASSES)[:, :, :, c]
+        def make_dy(t, c, halves=(0, 1)):
+            if (t, c) not in dy_tiles:
+                dy_tiles[(t, c)] = dy_pool.tile([P, CB, PACK], BF16, name="dy", align_bytes=64)
+            cols = slice(halves[0] * P, (halves[-1] + 1) * P)
+            dy = dy_tiles[(t, c)][:, cols, :]
+            g_c = g_sb[t][:].rearrange("p j (cb c) -> p j cb c", c=CLASSES)[:, :, cols, c]
             if c == 0:
-                nc.vector.tensor_copy(out=by_column(dy[:]), in_=by_token(g_c))
+                nc.vector.tensor_copy(out=by_column(dy), in_=by_token(g_c))
             else:
-                factor = (sin13[t][:, :, :, 0], cos2[t][:], factor3[t][:])[c - 1]
-                nc.vector.tensor_tensor(out=by_column(dy[:]), in0=by_token(factor), in1=by_token(g_c), op=ALU.mult)
-            made.append((t, c, dy))
+                factor = (sin13[t][:, :, cols, 0], cos2[t][:, :, cols], factor3[t][:, :, cols])[c - 1]
+                nc.vector.tensor_tensor(out=by_column(dy), in0=by_token(factor), in1=by_token(g_c), op=ALU.mult)
+            made.append((t, c, halves, cols, dy))
 
-        def multiply(t, c):
-            for h in range(HALVES):
+        def multiply(t, c, halves):
+            for h in halves:
                 cols = slice(h * P, (h + 1) * P)
                 nc.tensor.matmul_mx(
                     out=acc[c][h][:],
@@ -159,16 +165,16 @@ def tile_mylayerfunc_v_kernel(tc, x, weight, y, grad_out, out):
         x_ready = set()
 
         def quantise_dy():
-            t, c, dy = made.pop(0)
+            t, c, halves, cols, dy = made.pop(0)
             nc.vector.quantize_mx(
-                out=dy_codes[:, t, c, :].bitcast(E5M2X4),
-                scales=dy_scales[:, t, c, :],
-                in_=dy[:].rearrange("p cb j -> p (cb j)"),
+                out=dy_codes[:, t, c, cols].bitcast(E5M2X4),
+                scales=dy_scales[:, t, c, cols],
+                in_=dy.rearrange("p cb j -> p (cb j)"),
             )
             if t in x_ready:
-                multiply(t, c)
+                multiply(t, c, halves)
             else:
-                held.append((t, c))
+                held.append((t, c, halves))
 
         def quantise_x(t):
             nc.vector.quantize_mx(
@@ -180,67 +186,106 @@ def tile_mylayerfunc_v_kernel(tc, x, weight, y, grad_out, out):
             while held:
                 multiply(*held.pop(0))
 
-        def store(c, h, engine_copy):
+        def store(c, h, engine_copy, parts=1):
             res = results.tile([P, FEAT], F32, name="res")
-            engine_copy(out=res[:], in_=acc[c][h][:])
-            nc.sync.dma_start(out=out_dram[c][h * P : (h + 1) * P, :], in_=res[:])
+            width = FEAT // parts
+            for part in range(parts):
+                cols = slice(part * width, (part + 1) * width)
+                engine_copy(out=res[:, cols], in_=acc[c][h][:, cols])
+                nc.sync.dma_start(out=out_dram[c][h * P : (h + 1) * P, cols], in_=res[:, cols])
 
-        def make_first_three(t):
-            for c in range(3):
-                make_dy(t, c)
-
-        sines(0, FIRST)
-        sines(0, SECOND)
-        fourth_power(0)
-        make_first_three(0)
-        sines(1, FIRST)
+        absolute(0, FIRST)
+        sine(0, FIRST)
+        cosine(0, FIRST)
+        square(0, FIRST)
+        absolute(0, SECOND)
+        sine(0, SECOND)
+        fourth_power(0, FIRST)
+        square(0, SECOND)
+        cosine(0, SECOND)
+        fourth_power(0, SECOND)
+        make_dy(0, 0)
+        make_dy(0, 1)
+        make_dy(0, 2)
+        absolute(1, FIRST)
+        sine(1, FIRST)
+        square(1, FIRST)
+        cosine(1, FIRST)
+        fourth_power(1, FIRST)
+        quantise_dy()
+        quantise_dy()
+        quantise_dy()
         regroup_x(0)
-        quantise_dy()
-        quantise_dy()
-        quantise_x(0)
-        sines(1, SECOND)
-        fourth_power(1)
+        absolute(1, SECOND)
+        sine(1, SECOND)
+        cosine(1, SECOND)
+        square(1, SECOND)
+        fourth_power(1, SECOND)
         reciprocal(0)
         reciprocal(1)
-        quantise_dy()
+        quantise_x(0)
         regroup_x(1)
-        regroup_x(2)
         quantise_x(1)
-        quantise_x(2)
-        make_first_three(1)
-        sines(2, FIRST)
+        make_dy(1, 0)
+        make_dy(1, 1)
+        make_dy(1, 2)
         make_dy(0, 3)
-        sines(2, SECOND)
-        fourth_power(2)
-        quantise_dy()
         make_dy(1, 3)
         quantise_dy()
-        make_first_three(2)
-        sines(3, FIRST)
+        quantise_dy()
+        absolute(2, FIRST)
+        absolute(2, SECOND)
+        sine(2, FIRST)
+        sine(2, SECOND)
+        square(2, FIRST)
+        square(2, SECOND)
+        fourth_power(2, FIRST)
+        fourth_power(2, SECOND)
+        cosine(2, FIRST)
+        cosine(2, SECOND)
         quantise_dy()
         quantise_dy()
         quantise_dy()
-        sines(3, SECOND)
-        fourth_power(3)
+        regroup_x(2)
+        make_dy(2, 0)
+        make_dy(2, 1)
+        quantise_x(2)
+        absolute(3, FIRST)
+        sine(3, FIRST)
+        cosine(3, FIRST)
+        square(3, FIRST)
+        make_dy(2, 2)
+        quantise_dy()
+        quantise_dy()
+        absolute(3, SECOND)
+        sine(3, SECOND)
+        fourth_power(3, FIRST)
+        square(3, SECOND)
+        cosine(3, SECOND)
+        fourth_power(3, SECOND)
         reciprocal(2)
         reciprocal(3)
         quantise_dy()
-        quantise_dy()
         regroup_x(3)
-        quantise_dy()
         quantise_x(3)
-        make_first_three(3)
+        make_dy(3, 0)
+        make_dy(3, 1)
         quantise_dy()
+        make_dy(3, 2)
         quantise_dy()
+        store(0, 0, nc.vector.tensor_copy)
+        make_dy(2, 3, (0,))
         quantise_dy()
-        for c in range(2):
+        make_dy(2, 3, (1,))
+        quantise_dy()
+        store(0, 1, nc.scalar.copy)
+        for c in (1, 2):
             for h in range(HALVES):
                 store(c, h, nc.scalar.copy)
-        make_dy(2, 3)
-        make_dy(3, 3)
+        make_dy(3, 3, (0,))
         quantise_dy()
-        store(2, 0, nc.vector.tensor_copy)
-        store(2, 1, nc.scalar.copy)
+        make_dy(3, 3, (1,))
         quantise_dy()
-        store(3, 0, nc.vector.tensor_copy)
-        store(3, 1, nc.scalar.copy)
+        quantise_dy()
+        store(3, 0, nc.vector.tensor_copy, parts=2)
+        store(3, 1, nc.scalar.copy, parts=2)

@@ -264,21 +264,21 @@ def tile_mylayerfunc_v_kernel(tc, x, weight, y, grad_out, out):
         cosine(3, SECOND)
         fourth_power(3, SECOND)
         reciprocal(2)
-        reciprocal(3)
         quantise_dy()
         regroup_x(3)
-        quantise_x(3)
         make_dy(3, 0)
+        quantise_x(3)
         make_dy(3, 1)
         quantise_dy()
         make_dy(3, 2)
         quantise_dy()
         store(0, 0, nc.vector.tensor_copy)
+        store(0, 1, nc.scalar.copy)
+        reciprocal(3)
         make_dy(2, 3, (0,))
         quantise_dy()
         make_dy(2, 3, (1,))
         quantise_dy()
-        store(0, 1, nc.scalar.copy)
         for c in (1, 2):
             for h in range(HALVES):
                 store(c, h, nc.scalar.copy)

import math
from contextlib import ExitStack

import concourse.mybir as mybir

F32 = mybir.dt.float32
BF16 = mybir.dt.bfloat16
I32 = mybir.dt.int32
U32 = mybir.dt.uint32
U8 = mybir.dt.uint8
E4M3X4 = mybir.dt.float8_e4m3fn_x4
E5M2X4 = mybir.dt.float8_e5m2_x4
ACT = mybir.ActivationFunctionType
ALU = mybir.AluOpType

P = 128
PACK = 4
K_PASS = P * PACK
TOKENS = 2048
PASSES = TOKENS // K_PASS
COLS = 1024
CLASSES = 4
CB = COLS // CLASSES
FEAT = 512
HALVES = CB // P
RUN = 4

FLOPS = 2 * TOKENS * COLS * FEAT
BYTES = TOKENS * COLS * 4 + TOKENS * COLS * 2 + TOKENS * FEAT * 2 + COLS * FEAT * 4


def by_token(ap):
    return ap.rearrange("p j (m i) -> p m j i", i=RUN)


def by_column(ap):
    return ap.rearrange("p (m i) j -> p m j i", i=RUN)


def tile_mylayerfunc_v_kernel(tc, x, weight, y, grad_out, out):
    nc = tc.nc
    y_dram = y.rearrange("(t p j) n -> t p j n", p=P, j=PACK)
    g_dram = grad_out.rearrange("(t p j) n -> t p j n", p=P, j=PACK)
    x_dram = x.rearrange("(t p j) k -> t p j k", p=P, j=PACK)
    out_dram = out.rearrange("(cb c) k -> c cb k", c=CLASSES)

    with ExitStack() as stack:
        stack.enter_context(tc.manual_schedule())
        loads = stack.enter_context(tc.tile_pool(name="loads", bufs=1))
        keep = stack.enter_context(tc.tile_pool(name="keep", bufs=1))
        work = stack.enter_context(tc.tile_pool(name="work", bufs=2))
        dy_pool = stack.enter_context(tc.tile_pool(name="dy_pool", bufs=6))
        results = stack.enter_context(tc.tile_pool(name="results", bufs=8))
        psum = stack.enter_context(tc.psum_pool(name="psum", bufs=1))

        one = keep.tile([P, 1], F32, name="one")
        nc.vector.memset(one[:], 1.0)
        half_pi = keep.tile([P, 1], F32, name="half_pi")
        nc.vector.tensor_scalar(out=half_pi[:], in0=one[:], scalar1=math.pi / 2, scalar2=None, op0=ALU.mult)

        y_sb = [loads.tile([P, PACK, COLS], F32, name="y%d" % t) for t in range(PASSES)]
        g_sb = [loads.tile([P, PACK, COLS], BF16, name="g%d" % t) for t in range(PASSES)]
        x_sb = [loads.tile([P, PACK, FEAT], BF16, name="x%d" % t) for t in range(PASSES)]
        FIRST, SECOND = slice(0, 2), slice(2, 4)

        def load_y(t, js):
            nc.sync.dma_start(out=y_sb[t][:, js, :], in_=y_dram[t][:, js, :])

        def load_x(t):
            nc.sync.dma_start(out=x_sb[t][:], in_=x_dram[t])

        def load_g(t):
            nc.sync.dma_start(out=g_sb[t][:], in_=g_dram[t])

        load_y(0, FIRST)
        load_y(0, SECOND)
        load_g(0)
        load_y(1, FIRST)
        load_x(0)
        load_y(1, SECOND)
        load_x(1)
        load_g(1)
        for t in (2, 3):
            load_y(t, FIRST)
            load_y(t, SECOND)
            load_x(t)
            load_g(t)

        dy_codes = keep.tile([P, PASSES, CLASSES, CB], U32, name="dy_codes", align_bytes=64)
        dy_scales = keep.tile([P, PASSES, CLASSES, CB], U8, name="dy_scales", align_bytes=64)
        x_codes = keep.tile([P, PASSES, FEAT], U32, name="x_codes", align_bytes=64)
        x_scales = keep.tile([P, PASSES, FEAT], U8, name="x_scales", align_bytes=64)
        factor3 = [keep.tile([P, PACK, CB], F32, name="factor3_%d" % t) for t in range(PASSES)]
        acc = [
            [psum.tile([P, FEAT], F32, name="acc%d%d" % (c, h)) for h in range(HALVES)]
            for c in range(CLASSES)
        ]

        abs2, sin13, cos2, x_bf = {}, {}, {}, {}

        def absolute(t, js):
            if js == FIRST:
                abs2[t] = work.tile([P, PACK, CB], F32, name="abs2")
                sin13[t] = work.tile([P, PACK, CB, 2], F32, name="sin13")
                cos2[t] = work.tile([P, PACK, CB], F32, name="cos2")
            y4i = y_sb[t][:].bitcast(I32).rearrange("p j (cb c) -> p j cb c", c=CLASSES)
            nc.vector.tensor_scalar(
                out=abs2[t][:, js, :].bitcast(I32), in0=y4i[:, js, :, 2], scalar1=0x7FFFFFFF, scalar2=None, op0=ALU.bitwise_and
            )

        def sine(t, js):
            y4 = y_sb[t][:].rearrange("p j (cb c) -> p j cb c", c=CLASSES)
            nc.scalar.activation(out=sin13[t][:, js, :, :], in_=y4[:, js, :, 1::2], func=ACT.Sin, scale=-1.0)

        def cosine(t, js):
            nc.scalar.activation(
                out=cos2[t][:, js, :], in_=abs2[t][:, js, :], func=ACT.Sin, scale=-1.0, bias=half_pi[:]
            )

        def square(t, js):
            nc.scalar.activation(out=factor3[t][:, js, :], in_=sin13[t][:, js, :, 1], func=ACT.Square)

        def fourth_power(t, js):
            nc.scalar.activation(
                out=factor3[t][:, js, :], in_=factor3[t][:, js, :], func=ACT.Square, scale=-1.0, bias=one[:]
            )

        def reciprocal(t):
            nc.scalar.activation(out=factor3[t][:], in_=factor3[t][:], func=ACT.Abs_reciprocal_sqrt)

        def regroup_x(t):
            x_bf[t] = work.tile([P, FEAT, PACK], BF16, name="x_bf", align_bytes=64)
            nc.vector.tensor_copy(out=by_column(x_bf[t][:]), in_=by_token(x_sb[t][:]))

        made = []
        held = []
        dy_tiles = {}

        def make_dy(t, c, halves=(0, 1)):
            if (t, c) not in dy_tiles:
                dy_tiles[(t, c)] = dy_pool.tile([P, CB, PACK], BF16, name="dy", align_bytes=64)
            cols = slice(halves[0] * P, (halves[-1] + 1) * P)
            dy = dy_tiles[(t, c)][:, cols, :]
            g_c = g_sb[t][:].rearrange("p j (cb c) -> p j cb c", c=CLASSES)[:, :, cols, c]
            if c == 0:
                nc.vector.tensor_copy(out=by_column(dy), in_=by_token(g_c))
            else:
                factor = (sin13[t][:, :, cols, 0], cos2[t][:, :, cols], factor3[t][:, :, cols])[c - 1]
                nc.vector.tensor_tensor(out=by_column(dy), in0=by_token(factor), in1=by_token(g_c), op=ALU.mult)
            made.append((t, c, halves, cols, dy))

        def multiply(t, c, halves):
            for h in halves:
                cols = slice(h * P, (h + 1) * P)
                nc.tensor.matmul_mx(
                    out=acc[c][h][:],
                    lhsT=dy_codes[:, t, c, cols].bitcast(E5M2X4),
                    lhsT_scale=dy_scales[:, t, c, cols],
                    rhs=x_codes[:, t, :].bitcast(E4M3X4),
                    rhs_scale=x_scales[:, t, :],
                    start=(t == 0),
                    stop=(t == PASSES - 1),
                )

        x_ready = set()

        def quantise_dy():
            t, c, halves, cols, dy = made.pop(0)
            nc.vector.quantize_mx(
                out=dy_codes[:, t, c, cols].bitcast(E5M2X4),
                scales=dy_scales[:, t, c, cols],
                in_=dy.rearrange("p cb j -> p (cb j)"),
            )
            if t in x_ready:
                multiply(t, c, halves)
            else:
                held.append((t, c, halves))

        def quantise_x(t):
            nc.vector.quantize_mx(
                out=x_codes[:, t, :].bitcast(E4M3X4),
                scales=x_scales[:, t, :],
                in_=x_bf[t][:].rearrange("p k j -> p (k j)"),
            )
            x_ready.add(t)
            while held:
                multiply(*held.pop(0))

        def store(c, h, engine_copy, parts=1):
            res = results.tile([P, FEAT], F32, name="res")
            width = FEAT // parts
            for part in range(parts):
                cols = slice(part * width, (part + 1) * width)
                engine_copy(out=res[:, cols], in_=acc[c][h][:, cols])
                nc.sync.dma_start(out=out_dram[c][h * P : (h + 1) * P, cols], in_=res[:, cols])

        absolute(0, FIRST)
        sine(0, FIRST)
        cosine(0, FIRST)
        square(0, FIRST)
        absolute(0, SECOND)
        sine(0, SECOND)
        fourth_power(0, FIRST)
        square(0, SECOND)
        cosine(0, SECOND)
        fourth_power(0, SECOND)
        make_dy(0, 0)
        make_dy(0, 1)
        make_dy(0, 2)
        absolute(1, FIRST)
        sine(1, FIRST)
        square(1, FIRST)
        cosine(1, FIRST)
        fourth_power(1, FIRST)
        quantise_dy()
        quantise_dy()
        quantise_dy()
        regroup_x(0)
        absolute(1, SECOND)
        sine(1, SECOND)
        cosine(1, SECOND)
        square(1, SECOND)
        fourth_power(1, SECOND)
        reciprocal(0)
        reciprocal(1)
        quantise_x(0)
        regroup_x(1)
        quantise_x(1)
        make_dy(1, 0)
        make_dy(1, 1)
        make_dy(1, 2)
        make_dy(0, 3)
        make_dy(1, 3)
        quantise_dy()
        quantise_dy()
        absolute(2, FIRST)
        absolute(2, SECOND)
        sine(2, FIRST)
        sine(2, SECOND)
        square(2, FIRST)
        square(2, SECOND)
        fourth_power(2, FIRST)
        fourth_power(2, SECOND)
        cosine(2, FIRST)
        cosine(2, SECOND)
        quantise_dy()
        quantise_dy()
        quantise_dy()
        regroup_x(2)
        make_dy(2, 0)
        make_dy(2, 1)
        quantise_x(2)
        absolute(3, FIRST)
        sine(3, FIRST)
        cosine(3, FIRST)
        square(3, FIRST)
        make_dy(2, 2)
        quantise_dy()
        quantise_dy()
        absolute(3, SECOND)
        sine(3, SECOND)
        fourth_power(3, FIRST)
        square(3, SECOND)
        cosine(3, SECOND)
        fourth_power(3, SECOND)
        reciprocal(2)
        quantise_dy()
        regroup_x(3)
        make_dy(3, 0)
        quantise_x(3)
        make_dy(3, 1)
        quantise_dy()
        make_dy(3, 2)
        quantise_dy()
        store(0, 0, nc.vector.tensor_copy)
        store(0, 1, nc.scalar.copy)
        reciprocal(3)
        make_dy(2, 3, (0,))
        quantise_dy()
        make_dy(2, 3, (1,))
        quantise_dy()
        for c in (1, 2):
            for h in range(HALVES):
                store(c, h, nc.scalar.copy)
        make_dy(3, 3, (0,))
        quantise_dy()
        make_dy(3, 3, (1,))
        quantise_dy()
        quantise_dy()
        store(3, 0, nc.vector.tensor_copy, parts=2)
        store(3, 1, nc.scalar.copy, parts=2)
